import numpy as np
import ml_dtypes

BF16 = ml_dtypes.bfloat16


def bf(x):
    return np.asarray(x, np.float32).astype(BF16)


def f32(x):
    return np.asarray(x, np.float32)


def f64(x):
    return np.asarray(x).astype(np.float64)


def striped(idx):
    return np.tile(idx.reshape(-1, 16).T, (8, 1))


C, S, N, K, D0, D1, D2, D3 = 768, 2048, 2048, 4, 192, 384, 576, 768
DIMS = (D0, D1, D2, D3)


def setup_inputs():
    return {"table": f32(np.random.standard_normal((C, S))), "weights": f32(0.2 + 0.8 * np.random.random_sample((1, K))), "offs": striped(np.random.permutation(np.tile(np.arange(S), 2))[:N])}


def reference(table, weights, offs):
    idx = offs[:16].T.reshape(-1)
    mask = (np.arange(C)[None, :] < np.asarray(DIMS)[:, None]).astype(np.float64)
    scale = (f64(weights) @ mask).T
    return f64(table)[:, idx] * scale

@@ -1,0 +1,76 @@
+import concourse.mybir as mybir
+
+F32 = mybir.dt.float32
+I32 = mybir.dt.int32
+U16 = mybir.dt.uint16
+ALU = mybir.AluOpType
+COPY = mybir.ActivationFunctionType.Copy
+
+P = 128
+WIDTHS = (192, 384, 576, 768)
+PIECE = 512
+
+
+def tile_mixedembeddingv2_kernel(tc, table, weights, offs, out):
+    nc = tc.nc
+    features, words = table.shape
+    tokens = out.shape[1]
+    blocks = features // P
+    pieces = tokens // PIECE
+    candidates = len(WIDTHS)
+
+    with (
+        tc.tile_pool(name="held", bufs=1) as held,
+        tc.tile_pool(name="windows", bufs=blocks) as windows,
+        tc.tile_pool(name="factors", bufs=blocks) as factors,
+        tc.tile_pool(name="products", bufs=blocks * pieces) as products,
+    ):
+        offsets = held.tile([P, tokens // 16], U16, name="offsets")
+        nc.sync.dma_start(offsets[:], offs)
+
+        blend = held.tile([P, candidates], F32, name="blend")
+        nc.scalar.dma_start(blend[:], weights.broadcast_to([P, candidates]))
+
+        table_blocks = []
+        for b in range(blocks):
+            window = windows.tile([P, words], F32, name="window")
+            nc.sync.dma_start(window[:], table[b * P : (b + 1) * P, :])
+            table_blocks.append(window)
+
+        feature = held.tile([P, blocks], I32, name="feature")
+        nc.gpsimd.iota(feature[:], pattern=[[P, blocks]], base=0, channel_multiplier=1)
+
+        uses = held.tile([P, blocks, candidates], F32, name="uses")
+        for i, width in enumerate(WIDTHS):
+            nc.vector.tensor_single_scalar(uses[:, :, i], feature[:], float(width), ALU.is_lt)
+
+        weighted = held.tile([P, blocks, candidates], F32, name="weighted")
+        nc.vector.tensor_tensor(
+            weighted[:],
+            uses[:],
+            blend[:].unsqueeze(1).to_broadcast([P, blocks, candidates]),
+            ALU.mult,
+        )
+        scale = held.tile([P, blocks], F32, name="scale")
+        nc.vector.tensor_reduce(scale[:], weighted[:], axis=mybir.AxisListType.X, op=ALU.add)
+
+        scale_rows = []
+        for b in range(blocks):
+            factor = factors.tile([P, PIECE], F32, name="factor")
+            nc.scalar.activation(factor[:], scale[:, b : b + 1].to_broadcast([P, PIECE]), COPY)
+            scale_rows.append(factor)
+
+        for b in range(blocks):
+            for k in range(pieces):
+                product = products.tile([P, PIECE], F32, name="product")
+                nc.vector.tensor_tensor(
+                    product[:],
+                    table_blocks[b][:].indirect(
+                        offsets[:, k * (PIECE // 16) : (k + 1) * (PIECE // 16)]
+                    ),
+                    scale_rows[b][:],
+                    ALU.mult,
+                )
+                nc.scalar.dma_start(
+                    out[b * P : (b + 1) * P, k * PIECE : (k + 1) * PIECE], product[:]
+                )

@@ -25,16 +25,18 @@ def tile_mixedembeddingv2_kernel(tc, table, weights, offs, out):
         tc.tile_pool(name="factors", bufs=blocks) as factors,
         tc.tile_pool(name="products", bufs=blocks * pieces) as products,
     ):
-        offsets = held.tile([P, tokens // 16], U16, name="offsets")
-        nc.sync.dma_start(offsets[:], offs)
 
         blend = held.tile([P, candidates], F32, name="blend")
-        nc.scalar.dma_start(blend[:], weights.broadcast_to([P, candidates]))
+        nc.sync.dma_start(blend[:], weights.broadcast_to([P, candidates]))
+
+        offsets = held.tile([P, tokens // 16], U16, name="offsets")
+        nc.sync.dma_start(offsets[:], offs)
 
         table_blocks = []
         for b in range(blocks):
             window = windows.tile([P, words], F32, name="window")
-            nc.sync.dma_start(window[:], table[b * P : (b + 1) * P, :])
+            load_queue = nc.scalar if b == 0 else nc.sync
+            load_queue.dma_start(window[:], table[b * P : (b + 1) * P, :])
             table_blocks.append(window)
 
         feature = held.tile([P, blocks], I32, name="feature")
@@ -57,7 +59,11 @@ def tile_mixedembeddingv2_kernel(tc, table, weights, offs, out):
         scale_rows = []
         for b in range(blocks):
             factor = factors.tile([P, PIECE], F32, name="factor")
-            nc.scalar.activation(factor[:], scale[:, b : b + 1].to_broadcast([P, PIECE]), COPY)
+            repeated = scale[:, b : b + 1].to_broadcast([P, PIECE])
+            if b == 0:
+                nc.vector.tensor_copy(factor[:], repeated)
+            else:
+                nc.scalar.activation(factor[:], repeated, COPY)
             scale_rows.append(factor)
 
         for b in range(blocks):

@@ -25,18 +25,16 @@ def tile_mixedembeddingv2_kernel(tc, table, weights, offs, out):
         tc.tile_pool(name="factors", bufs=blocks) as factors,
         tc.tile_pool(name="products", bufs=blocks * pieces) as products,
     ):
-
-        blend = held.tile([P, candidates], F32, name="blend")
-        nc.sync.dma_start(blend[:], weights.broadcast_to([P, candidates]))
-
         offsets = held.tile([P, tokens // 16], U16, name="offsets")
         nc.sync.dma_start(offsets[:], offs)
+
+        blend = held.tile([P, candidates], F32, name="blend")
+        nc.scalar.dma_start(blend[:], weights.broadcast_to([P, candidates]))
 
         table_blocks = []
         for b in range(blocks):
             window = windows.tile([P, words], F32, name="window")
-            load_queue = nc.scalar if b == 0 else nc.sync
-            load_queue.dma_start(window[:], table[b * P : (b + 1) * P, :])
+            nc.sync.dma_start(window[:], table[b * P : (b + 1) * P, :])
             table_blocks.append(window)
 
         feature = held.tile([P, blocks], I32, name="feature")
@@ -59,11 +57,7 @@ def tile_mixedembeddingv2_kernel(tc, table, weights, offs, out):
         scale_rows = []
         for b in range(blocks):
             factor = factors.tile([P, PIECE], F32, name="factor")
-            repeated = scale[:, b : b + 1].to_broadcast([P, PIECE])
-            if b == 0:
-                nc.vector.tensor_copy(factor[:], repeated)
-            else:
-                nc.scalar.activation(factor[:], repeated, COPY)
+            nc.scalar.activation(factor[:], scale[:, b : b + 1].to_broadcast([P, PIECE]), COPY)
             scale_rows.append(factor)
 
         for b in range(blocks):
@@ -77,6 +71,6 @@ def tile_mixedembeddingv2_kernel(tc, table, weights, offs, out):
                     scale_rows[b][:],
                     ALU.mult,
                 )
-                nc.scalar.dma_start(
+                nc.sync.dma_start(
                     out[b * P : (b + 1) * P, k * PIECE : (k + 1) * PIECE], product[:]
                 )

@@ -8,7 +8,18 @@ COPY = mybir.ActivationFunctionType.Copy
 
 P = 128
 WIDTHS = (192, 384, 576, 768)
-PIECE = 512
+FIRST_PIECE = 512
+LAST_PIECE = 128
+
+
+def halving(total, smallest):
+    pieces = []
+    left = total
+    while left > smallest:
+        pieces.append(left // 2)
+        left -= left // 2
+    pieces.append(left)
+    return pieces
 
 
 def tile_mixedembeddingv2_kernel(tc, table, weights, offs, out):
@@ -16,14 +27,17 @@ def tile_mixedembeddingv2_kernel(tc, table, weights, offs, out):
     features, words = table.shape
     tokens = out.shape[1]
     blocks = features // P
-    pieces = tokens // PIECE
     candidates = len(WIDTHS)
+
+    cuts = [[FIRST_PIECE] * (tokens // FIRST_PIECE)]
+    cuts.extend([tokens] for b in range(1, blocks - 1))
+    cuts.append(halving(tokens, LAST_PIECE))
 
     with (
         tc.tile_pool(name="held", bufs=1) as held,
         tc.tile_pool(name="windows", bufs=blocks) as windows,
         tc.tile_pool(name="factors", bufs=blocks) as factors,
-        tc.tile_pool(name="products", bufs=blocks * pieces) as products,
+        tc.tile_pool(name="products", bufs=blocks) as products,
     ):
         offsets = held.tile([P, tokens // 16], U16, name="offsets")
         nc.sync.dma_start(offsets[:], offs)
@@ -56,21 +70,21 @@ def tile_mixedembeddingv2_kernel(tc, table, weights, offs, out):
 
         scale_rows = []
         for b in range(blocks):
-            factor = factors.tile([P, PIECE], F32, name="factor")
-            nc.scalar.activation(factor[:], scale[:, b : b + 1].to_broadcast([P, PIECE]), COPY)
+            widest = max(cuts[b])
+            factor = factors.tile([P, widest], F32, name="factor")
+            nc.scalar.activation(factor[:], scale[:, b : b + 1].to_broadcast([P, widest]), COPY)
             scale_rows.append(factor)
 
         for b in range(blocks):
-            for k in range(pieces):
-                product = products.tile([P, PIECE], F32, name="product")
+            product = products.tile([P, tokens], F32, name="product")
+            start = 0
+            for width in cuts[b]:
+                stop = start + width
                 nc.vector.tensor_tensor(
-                    product[:],
-                    table_blocks[b][:].indirect(
-                        offsets[:, k * (PIECE // 16) : (k + 1) * (PIECE // 16)]
-                    ),
-                    scale_rows[b][:],
+                    product[:, start:stop],
+                    table_blocks[b][:].indirect(offsets[:, start // 16 : stop // 16]),
+                    scale_rows[b][:, 0:width],
                     ALU.mult,
                 )
-                nc.sync.dma_start(
-                    out[b * P : (b + 1) * P, k * PIECE : (k + 1) * PIECE], product[:]
-                )
+                nc.sync.dma_start(out[b * P : (b + 1) * P, start:stop], product[:, start:stop])
+                start = stop

@@ -29,6 +29,10 @@ def tile_mixedembeddingv2_kernel(tc, table, weights, offs, out):
     blocks = features // P
     candidates = len(WIDTHS)
 
+    assert all(width % blocks == 0 for width in WIDTHS)
+    table_by_block = table.rearrange("(p b) s -> p b s", b=blocks)
+    out_by_block = out.rearrange("(p b) j -> p b j", b=blocks)
+
     cuts = [[FIRST_PIECE] * (tokens // FIRST_PIECE)]
     cuts.extend([tokens] for b in range(1, blocks - 1))
     cuts.append(halving(tokens, LAST_PIECE))
@@ -36,7 +40,6 @@ def tile_mixedembeddingv2_kernel(tc, table, weights, offs, out):
     with (
         tc.tile_pool(name="held", bufs=1) as held,
         tc.tile_pool(name="windows", bufs=blocks) as windows,
-        tc.tile_pool(name="factors", bufs=blocks) as factors,
         tc.tile_pool(name="products", bufs=blocks) as products,
     ):
         offsets = held.tile([P, tokens // 16], U16, name="offsets")
@@ -48,32 +51,29 @@ def tile_mixedembeddingv2_kernel(tc, table, weights, offs, out):
         table_blocks = []
         for b in range(blocks):
             window = windows.tile([P, words], F32, name="window")
-            nc.sync.dma_start(window[:], table[b * P : (b + 1) * P, :])
+            nc.sync.dma_start(window[:], table_by_block[:, b, :])
             table_blocks.append(window)
 
-        feature = held.tile([P, blocks], I32, name="feature")
-        nc.gpsimd.iota(feature[:], pattern=[[P, blocks]], base=0, channel_multiplier=1)
-
-        uses = held.tile([P, blocks, candidates], F32, name="uses")
+        partition = held.tile([P, 1], I32, name="partition")
+        nc.gpsimd.iota(partition[:], pattern=[[0, 1]], base=0, channel_multiplier=1)
+        uses = held.tile([P, candidates], F32, name="uses")
         for i, width in enumerate(WIDTHS):
-            nc.vector.tensor_single_scalar(uses[:, :, i], feature[:], float(width), ALU.is_lt)
+            nc.vector.tensor_single_scalar(
+                uses[:, i : i + 1], partition[:], float(width // blocks), ALU.is_lt
+            )
 
-        weighted = held.tile([P, blocks, candidates], F32, name="weighted")
-        nc.vector.tensor_tensor(
-            weighted[:],
-            uses[:],
-            blend[:].unsqueeze(1).to_broadcast([P, blocks, candidates]),
-            ALU.mult,
-        )
-        scale = held.tile([P, blocks], F32, name="scale")
+        weighted = held.tile([P, candidates], F32, name="weighted")
+        nc.vector.tensor_tensor(weighted[:], uses[:], blend[:], ALU.mult)
+        scale = held.tile([P, 1], F32, name="scale")
         nc.vector.tensor_reduce(scale[:], weighted[:], axis=mybir.AxisListType.X, op=ALU.add)
 
-        scale_rows = []
-        for b in range(blocks):
-            widest = max(cuts[b])
-            factor = factors.tile([P, widest], F32, name="factor")
-            nc.scalar.activation(factor[:], scale[:, b : b + 1].to_broadcast([P, widest]), COPY)
-            scale_rows.append(factor)
+        factor = held.tile([P, tokens], F32, name="factor")
+        for start in range(0, tokens, FIRST_PIECE):
+            nc.scalar.activation(
+                factor[:, start : start + FIRST_PIECE],
+                scale[:].to_broadcast([P, FIRST_PIECE]),
+                COPY,
+            )
 
         for b in range(blocks):
             product = products.tile([P, tokens], F32, name="product")
@@ -83,8 +83,8 @@ def tile_mixedembeddingv2_kernel(tc, table, weights, offs, out):
                 nc.vector.tensor_tensor(
                     product[:, start:stop],
                     table_blocks[b][:].indirect(offsets[:, start // 16 : stop // 16]),
-                    scale_rows[b][:, 0:width],
+                    factor[:, start:stop],
                     ALU.mult,
                 )
-                nc.sync.dma_start(out[b * P : (b + 1) * P, start:stop], product[:, start:stop])
+                nc.sync.dma_start(out_by_block[:, b, start:stop], product[:, start:stop])
                 start = stop

@@ -1,7 +1,6 @@
 import concourse.mybir as mybir
 
 F32 = mybir.dt.float32
-I32 = mybir.dt.int32
 U16 = mybir.dt.uint16
 ALU = mybir.AluOpType
 COPY = mybir.ActivationFunctionType.Copy
@@ -54,13 +53,10 @@ def tile_mixedembeddingv2_kernel(tc, table, weights, offs, out):
             nc.sync.dma_start(window[:], table_by_block[:, b, :])
             table_blocks.append(window)
 
-        partition = held.tile([P, 1], I32, name="partition")
-        nc.gpsimd.iota(partition[:], pattern=[[0, 1]], base=0, channel_multiplier=1)
         uses = held.tile([P, candidates], F32, name="uses")
+        nc.vector.memset(uses[:], 0.0)
         for i, width in enumerate(WIDTHS):
-            nc.vector.tensor_single_scalar(
-                uses[:, i : i + 1], partition[:], float(width // blocks), ALU.is_lt
-            )
+            nc.vector.memset(uses[0 : width // blocks, i : i + 1], 1.0)
 
         weighted = held.tile([P, candidates], F32, name="weighted")
         nc.vector.tensor_tensor(weighted[:], uses[:], blend[:], ALU.mult)
@@ -68,7 +64,8 @@ def tile_mixedembeddingv2_kernel(tc, table, weights, offs, out):
         nc.vector.tensor_reduce(scale[:], weighted[:], axis=mybir.AxisListType.X, op=ALU.add)
 
         factor = held.tile([P, tokens], F32, name="factor")
-        for start in range(0, tokens, FIRST_PIECE):
+        nc.vector.tensor_copy(factor[:, 0:FIRST_PIECE], scale[:].to_broadcast([P, FIRST_PIECE]))
+        for start in range(FIRST_PIECE, tokens, FIRST_PIECE):
             nc.scalar.activation(
                 factor[:, start : start + FIRST_PIECE],
                 scale[:].to_broadcast([P, FIRST_PIECE]),

@@ -41,11 +41,11 @@ def tile_mixedembeddingv2_kernel(tc, table, weights, offs, out):
         tc.tile_pool(name="windows", bufs=blocks) as windows,
         tc.tile_pool(name="products", bufs=blocks) as products,
     ):
+        blend = held.tile([P, candidates], F32, name="blend")
+        nc.sync.dma_start(blend[:], weights.broadcast_to([P, candidates]))
+
         offsets = held.tile([P, tokens // 16], U16, name="offsets")
         nc.sync.dma_start(offsets[:], offs)
-
-        blend = held.tile([P, candidates], F32, name="blend")
-        nc.scalar.dma_start(blend[:], weights.broadcast_to([P, candidates]))
 
         table_blocks = []
         for b in range(blocks):

@@ -8,7 +8,7 @@ COPY = mybir.ActivationFunctionType.Copy
 P = 128
 WIDTHS = (192, 384, 576, 768)
 FIRST_PIECE = 512
-LAST_PIECE = 128
+LAST_PIECE = 256
 
 
 def halving(total, smallest):

@@ -7,7 +7,6 @@ COPY = mybir.ActivationFunctionType.Copy
 
 P = 128
 WIDTHS = (192, 384, 576, 768)
-FIRST_PIECE = 512
 LAST_PIECE = 256
 
 
@@ -32,8 +31,7 @@ def tile_mixedembeddingv2_kernel(tc, table, weights, offs, out):
     table_by_block = table.rearrange("(p b) s -> p b s", b=blocks)
     out_by_block = out.rearrange("(p b) j -> p b j", b=blocks)
 
-    cuts = [[FIRST_PIECE] * (tokens // FIRST_PIECE)]
-    cuts.extend([tokens] for b in range(1, blocks - 1))
+    cuts = [[tokens] for b in range(blocks - 1)]
     cuts.append(halving(tokens, LAST_PIECE))
 
     with (
@@ -64,13 +62,9 @@ def tile_mixedembeddingv2_kernel(tc, table, weights, offs, out):
         nc.vector.tensor_reduce(scale[:], weighted[:], axis=mybir.AxisListType.X, op=ALU.add)
 
         factor = held.tile([P, tokens], F32, name="factor")
-        nc.vector.tensor_copy(factor[:, 0:FIRST_PIECE], scale[:].to_broadcast([P, FIRST_PIECE]))
-        for start in range(FIRST_PIECE, tokens, FIRST_PIECE):
-            nc.scalar.activation(
-                factor[:, start : start + FIRST_PIECE],
-                scale[:].to_broadcast([P, FIRST_PIECE]),
-                COPY,
-            )
+        half = tokens // 2
+        nc.vector.tensor_copy(factor[:, 0:half], scale[:].to_broadcast([P, half]))
+        nc.scalar.activation(factor[:, half:tokens], scale[:].to_broadcast([P, half]), COPY)
 
         for b in range(blocks):
             product = products.tile([P, tokens], F32, name="product")

@@ -77,5 +77,10 @@ def tile_mixedembeddingv2_kernel(tc, table, weights, offs, out):
                     factor[:, start:stop],
                     ALU.mult,
                 )
-                nc.sync.dma_start(out_by_block[:, b, start:stop], product[:, start:stop])
+                stores = 2 if b == 0 else 1
+                step = width // stores
+                for left in range(start, stop, step):
+                    nc.sync.dma_start(
+                        out_by_block[:, b, left : left + step], product[:, left : left + step]
+                    )
                 start = stop

@@ -57,9 +57,10 @@ def tile_mixedembeddingv2_kernel(tc, table, weights, offs, out):
             nc.vector.memset(uses[0 : width // blocks, i : i + 1], 1.0)
 
         weighted = held.tile([P, candidates], F32, name="weighted")
-        nc.vector.tensor_tensor(weighted[:], uses[:], blend[:], ALU.mult)
         scale = held.tile([P, 1], F32, name="scale")
-        nc.vector.tensor_reduce(scale[:], weighted[:], axis=mybir.AxisListType.X, op=ALU.add)
+        nc.vector.scalar_tensor_tensor(
+            weighted[:], uses[:], 1.0, blend[:], ALU.mult, ALU.mult, accum_out=scale[:]
+        )
 
         factor = held.tile([P, tokens], F32, name="factor")
         half = tokens // 2

@@ -7,7 +7,7 @@ COPY = mybir.ActivationFunctionType.Copy
 
 P = 128
 WIDTHS = (192, 384, 576, 768)
-LAST_PIECE = 256
+LAST_PIECE = 128
 
 
 def halving(total, smallest):
@@ -78,10 +78,5 @@ def tile_mixedembeddingv2_kernel(tc, table, weights, offs, out):
                     factor[:, start:stop],
                     ALU.mult,
                 )
-                stores = 2 if b == 0 else 1
-                step = width // stores
-                for left in range(start, stop, step):
-                    nc.sync.dma_start(
-                        out_by_block[:, b, left : left + step], product[:, left : left + step]
-                    )
+                nc.sync.dma_start(out_by_block[:, b, start:stop], product[:, start:stop])
                 start = stop

@@ -7,6 +7,7 @@ COPY = mybir.ActivationFunctionType.Copy
 
 P = 128
 WIDTHS = (192, 384, 576, 768)
+ALIGN = 256
 LAST_PIECE = 128
 
 
@@ -42,12 +43,12 @@ def tile_mixedembeddingv2_kernel(tc, table, weights, offs, out):
         blend = held.tile([P, candidates], F32, name="blend")
         nc.sync.dma_start(blend[:], weights.broadcast_to([P, candidates]))
 
-        offsets = held.tile([P, tokens // 16], U16, name="offsets")
+        offsets = held.tile([P, tokens // 16], U16, name="offsets", align_bytes=ALIGN)
         nc.sync.dma_start(offsets[:], offs)
 
         table_blocks = []
         for b in range(blocks):
-            window = windows.tile([P, words], F32, name="window")
+            window = windows.tile([P, words], F32, name="window", align_bytes=ALIGN)
             nc.sync.dma_start(window[:], table_by_block[:, b, :])
             table_blocks.append(window)
 
@@ -62,13 +63,13 @@ def tile_mixedembeddingv2_kernel(tc, table, weights, offs, out):
             weighted[:], uses[:], 1.0, blend[:], ALU.mult, ALU.mult, accum_out=scale[:]
         )
 
-        factor = held.tile([P, tokens], F32, name="factor")
+        factor = held.tile([P, tokens], F32, name="factor", align_bytes=ALIGN)
         half = tokens // 2
         nc.vector.tensor_copy(factor[:, 0:half], scale[:].to_broadcast([P, half]))
         nc.scalar.activation(factor[:, half:tokens], scale[:].to_broadcast([P, half]), COPY)
 
         for b in range(blocks):
-            product = products.tile([P, tokens], F32, name="product")
+            product = products.tile([P, tokens], F32, name="product", align_bytes=ALIGN)
             start = 0
             for width in cuts[b]:
                 stop = start + width

@@ -3,7 +3,6 @@ import concourse.mybir as mybir
 F32 = mybir.dt.float32
 U16 = mybir.dt.uint16
 ALU = mybir.AluOpType
-COPY = mybir.ActivationFunctionType.Copy
 
 P = 128
 WIDTHS = (192, 384, 576, 768)
@@ -64,9 +63,7 @@ def tile_mixedembeddingv2_kernel(tc, table, weights, offs, out):
         )
 
         factor = held.tile([P, tokens], F32, name="factor", align_bytes=ALIGN)
-        half = tokens // 2
-        nc.vector.tensor_copy(factor[:, 0:half], scale[:].to_broadcast([P, half]))
-        nc.scalar.activation(factor[:, half:tokens], scale[:].to_broadcast([P, half]), COPY)
+        nc.vector.tensor_copy(factor[:], scale[:].to_broadcast([P, tokens]))
 
         for b in range(blocks):
             product = products.tile([P, tokens], F32, name="product", align_bytes=ALIGN)

@@ -7,6 +7,8 @@ ALU = mybir.AluOpType
 P = 128
 WIDTHS = (192, 384, 576, 768)
 ALIGN = 256
+STORE_PIECE = 512
+SPLIT_BLOCKS = 2
 LAST_PIECE = 128
 
 
@@ -76,5 +78,9 @@ def tile_mixedembeddingv2_kernel(tc, table, weights, offs, out):
                     factor[:, start:stop],
                     ALU.mult,
                 )
-                nc.sync.dma_start(out_by_block[:, b, start:stop], product[:, start:stop])
+                step = STORE_PIECE if b < SPLIT_BLOCKS else width
+                for left in range(start, stop, step):
+                    nc.sync.dma_start(
+                        out_by_block[:, b, left : left + step], product[:, left : left + step]
+                    )
                 start = stop

import concourse.mybir as mybir

F32 = mybir.dt.float32
U16 = mybir.dt.uint16
ALU = mybir.AluOpType

P = 128
WIDTHS = (192, 384, 576, 768)
ALIGN = 256
STORE_PIECE = 512
SPLIT_BLOCKS = 2
LAST_PIECE = 128


def halving(total, smallest):
    pieces = []
    left = total
    while left > smallest:
        pieces.append(left // 2)
        left -= left // 2
    pieces.append(left)
    return pieces


def tile_mixedembeddingv2_kernel(tc, table, weights, offs, out):
    nc = tc.nc
    features, words = table.shape
    tokens = out.shape[1]
    blocks = features // P
    candidates = len(WIDTHS)

    assert all(width % blocks == 0 for width in WIDTHS)
    table_by_block = table.rearrange("(p b) s -> p b s", b=blocks)
    out_by_block = out.rearrange("(p b) j -> p b j", b=blocks)

    cuts = [[tokens] for b in range(blocks - 1)]
    cuts.append(halving(tokens, LAST_PIECE))

    with (
        tc.tile_pool(name="held", bufs=1) as held,
        tc.tile_pool(name="windows", bufs=blocks) as windows,
        tc.tile_pool(name="products", bufs=blocks) as products,
    ):
        blend = held.tile([P, candidates], F32, name="blend")
        nc.sync.dma_start(blend[:], weights.broadcast_to([P, candidates]))

        offsets = held.tile([P, tokens // 16], U16, name="offsets", align_bytes=ALIGN)
        nc.sync.dma_start(offsets[:], offs)

        table_blocks = []
        for b in range(blocks):
            window = windows.tile([P, words], F32, name="window", align_bytes=ALIGN)
            nc.sync.dma_start(window[:], table_by_block[:, b, :])
            table_blocks.append(window)

        uses = held.tile([P, candidates], F32, name="uses")
        nc.vector.memset(uses[:], 0.0)
        for i, width in enumerate(WIDTHS):
            nc.vector.memset(uses[0 : width // blocks, i : i + 1], 1.0)

        weighted = held.tile([P, candidates], F32, name="weighted")
        scale = held.tile([P, 1], F32, name="scale")
        nc.vector.scalar_tensor_tensor(
            weighted[:], uses[:], 1.0, blend[:], ALU.mult, ALU.mult, accum_out=scale[:]
        )

        factor = held.tile([P, tokens], F32, name="factor", align_bytes=ALIGN)
        nc.vector.tensor_copy(factor[:], scale[:].to_broadcast([P, tokens]))

        for b in range(blocks):
            product = products.tile([P, tokens], F32, name="product", align_bytes=ALIGN)
            start = 0
            for width in cuts[b]:
                stop = start + width
                nc.vector.tensor_tensor(
                    product[:, start:stop],
                    table_blocks[b][:].indirect(offsets[:, start // 16 : stop // 16]),
                    factor[:, start:stop],
                    ALU.mult,
                )
                step = STORE_PIECE if b < SPLIT_BLOCKS else width
                for left in range(start, stop, step):
                    nc.sync.dma_start(
                        out_by_block[:, b, left : left + step], product[:, left : left + step]
                    )
                start = stop
